import numpy as np
import ml_dtypes

BF16 = ml_dtypes.bfloat16


def bf(x):
    return np.asarray(x, np.float32).astype(BF16)


def f32(x):
    return np.asarray(x, np.float32)


def f64(x):
    return np.asarray(x).astype(np.float64)


def striped(idx):
    return np.tile(idx.reshape(-1, 16).T, (8, 1))


V, D, N = 4096, 128, 2048


def setup_inputs():
    return {"table": bf(0.5 * np.random.standard_normal((V, D))), "w_a": bf(np.random.standard_normal((D, D)) / np.sqrt(D)), "w_o": bf(np.random.standard_normal((D, D)) / np.sqrt(D)), "offs": striped(np.random.permutation(np.tile(np.arange(V), 2))[:N])}


def reference(table, w_a, w_o, offs):
    idx = offs[:16].T.reshape(-1)
    xt = f64(table)[idx].T
    return np.concatenate([f64(w_a).T @ xt, f64(w_o).T @ xt], axis=0)

@@ -1,0 +1,72 @@
+import concourse.mybir as mybir
+from concourse.masks import make_identity
+
+V, D, N = 4096, 128, 2048
+P = 128
+PIECE = 512
+BLOCKS = V // P
+GROUP = 8
+
+BF16, F32, U16 = mybir.dt.bfloat16, mybir.dt.float32, mybir.dt.uint16
+
+FLOPS = 2 * D * (2 * D) * N
+
+
+def tile_wsdmodel_kernel(tc, table, w_a, w_o, offs, out):
+    nc = tc.nc
+    with (
+        tc.tile_pool(name="held", bufs=1) as held,
+        tc.tile_pool(name="staging", bufs=4) as staging,
+        tc.psum_pool(name="flip_banks", bufs=2) as flip_banks,
+        tc.psum_pool(name="product_banks", bufs=3) as product_banks,
+    ):
+        offsets = held.tile([P, N // 16], U16, name="offsets")
+        nc.sync.dma_start(offsets[:], offs)
+
+        words = held.tile([P, BLOCKS, D], BF16, name="words")
+        table_blocks = table.rearrange("(b p) d -> p b d", p=P)
+        for g in range(BLOCKS // GROUP):
+            queue = nc.sync if g % 2 == 0 else nc.scalar
+            blocks = slice(g * GROUP, (g + 1) * GROUP)
+            queue.dma_start(words[:, blocks, :], table_blocks[:, blocks, :])
+
+        weights_a = held.tile([D, D], BF16, name="weights_a")
+        nc.sync.dma_start(weights_a[:], w_a)
+        weights_o = held.tile([D, D], BF16, name="weights_o")
+        nc.scalar.dma_start(weights_o[:], w_o)
+
+        identity = held.tile([P, P], BF16, name="identity")
+        make_identity(nc, identity[:])
+
+        window = held.tile([D, V], BF16, name="window")
+        for g in range(BLOCKS // GROUP):
+            flipped = flip_banks.tile([D, GROUP * P], BF16, name="flipped")
+            for k in range(GROUP):
+                nc.tensor.transpose(
+                    flipped[:, k * P : (k + 1) * P], words[:, g * GROUP + k, :], identity[:]
+                )
+            columns = window[:, g * GROUP * P : (g + 1) * GROUP * P]
+            if g % 2 == 0:
+                nc.vector.tensor_copy(columns, flipped[:])
+            else:
+                nc.scalar.copy(columns, flipped[:])
+
+        for piece in range(N // PIECE):
+            piece_offsets = offsets[:, piece * (PIECE // 16) : (piece + 1) * (PIECE // 16)]
+            piece_columns = slice(piece * PIECE, (piece + 1) * PIECE)
+
+            product_a = product_banks.tile([D, PIECE], F32, name="product_a")
+            nc.tensor.matmul(
+                product_a[:], weights_a[:], window[:].indirect(piece_offsets), start=True, stop=True
+            )
+            staged_a = staging.tile([D, PIECE], F32, name="staged_a")
+            nc.vector.tensor_copy(staged_a[:], product_a[:])
+            nc.sync.dma_start(out[0:D, piece_columns], staged_a[:])
+
+            product_o = product_banks.tile([D, PIECE], F32, name="product_o")
+            nc.tensor.matmul(
+                product_o[:], weights_o[:], window[:].indirect(piece_offsets), start=True, stop=True
+            )
+            staged_o = staging.tile([D, PIECE], F32, name="staged_o")
+            nc.scalar.copy(staged_o[:], product_o[:])
+            nc.scalar.dma_start(out[D : 2 * D, piece_columns], staged_o[:])

@@ -5,7 +5,7 @@ V, D, N = 4096, 128, 2048
 P = 128
 PIECE = 512
 BLOCKS = V // P
-GROUP = 8
+GROUP = 4
 
 BF16, F32, U16 = mybir.dt.bfloat16, mybir.dt.float32, mybir.dt.uint16
 
@@ -17,12 +17,9 @@ def tile_wsdmodel_kernel(tc, table, w_a, w_o, offs, out):
     with (
         tc.tile_pool(name="held", bufs=1) as held,
         tc.tile_pool(name="staging", bufs=4) as staging,
-        tc.psum_pool(name="flip_banks", bufs=2) as flip_banks,
-        tc.psum_pool(name="product_banks", bufs=3) as product_banks,
+        tc.psum_pool(name="flip_banks", bufs=4) as flip_banks,
+        tc.psum_pool(name="product_banks", bufs=2) as product_banks,
     ):
-        offsets = held.tile([P, N // 16], U16, name="offsets")
-        nc.sync.dma_start(offsets[:], offs)
-
         words = held.tile([P, BLOCKS, D], BF16, name="words")
         table_blocks = table.rearrange("(b p) d -> p b d", p=P)
         for g in range(BLOCKS // GROUP):
@@ -30,6 +27,8 @@ def tile_wsdmodel_kernel(tc, table, w_a, w_o, offs, out):
             blocks = slice(g * GROUP, (g + 1) * GROUP)
             queue.dma_start(words[:, blocks, :], table_blocks[:, blocks, :])
 
+        offsets = held.tile([P, N // 16], U16, name="offsets")
+        nc.sync.dma_start(offsets[:], offs)
         weights_a = held.tile([D, D], BF16, name="weights_a")
         nc.sync.dma_start(weights_a[:], w_a)
         weights_o = held.tile([D, D], BF16, name="weights_o")

@@ -4,8 +4,8 @@ from concourse.masks import make_identity
 V, D, N = 4096, 128, 2048
 P = 128
 PIECE = 512
-BLOCKS = V // P
-GROUP = 4
+RUN = 4
+GROUPS = V // (P * RUN)
 
 BF16, F32, U16 = mybir.dt.bfloat16, mybir.dt.float32, mybir.dt.uint16
 
@@ -20,35 +20,36 @@ def tile_wsdmodel_kernel(tc, table, w_a, w_o, offs, out):
         tc.psum_pool(name="flip_banks", bufs=4) as flip_banks,
         tc.psum_pool(name="product_banks", bufs=2) as product_banks,
     ):
-        words = held.tile([P, BLOCKS, D], BF16, name="words")
-        table_blocks = table.rearrange("(b p) d -> p b d", p=P)
-        for g in range(BLOCKS // GROUP):
-            queue = nc.sync if g % 2 == 0 else nc.scalar
-            blocks = slice(g * GROUP, (g + 1) * GROUP)
-            queue.dma_start(words[:, blocks, :], table_blocks[:, blocks, :])
-
         offsets = held.tile([P, N // 16], U16, name="offsets")
         nc.sync.dma_start(offsets[:], offs)
-        weights_a = held.tile([D, D], BF16, name="weights_a")
-        nc.sync.dma_start(weights_a[:], w_a)
-        weights_o = held.tile([D, D], BF16, name="weights_o")
-        nc.scalar.dma_start(weights_o[:], w_o)
+
+        words = held.tile([P, GROUPS, RUN * D], BF16, name="words")
+        table_runs = table.rearrange("(g p k) d -> p g (k d)", p=P, k=RUN)
+        for g in range(GROUPS):
+            queue = nc.sync if g % 2 == 0 else nc.scalar
+            queue.dma_start(words[:, g, :], table_runs[:, g, :])
 
         identity = held.tile([P, P], BF16, name="identity")
         make_identity(nc, identity[:])
 
+        weights_a = held.tile([D, D], BF16, name="weights_a")
+        nc.gpsimd.dma_start(weights_a[:], w_a)
+        weights_o = held.tile([D, D], BF16, name="weights_o")
+        nc.gpsimd.dma_start(weights_o[:], w_o)
+
         window = held.tile([D, V], BF16, name="window")
-        for g in range(BLOCKS // GROUP):
-            flipped = flip_banks.tile([D, GROUP * P], BF16, name="flipped")
-            for k in range(GROUP):
+        for g in range(GROUPS):
+            flipped = flip_banks.tile([D, RUN * P], BF16, name="flipped")
+            for k in range(RUN):
                 nc.tensor.transpose(
-                    flipped[:, k * P : (k + 1) * P], words[:, g * GROUP + k, :], identity[:]
+                    flipped[:, k * P : (k + 1) * P], words[:, g, k * D : (k + 1) * D], identity[:]
                 )
-            columns = window[:, g * GROUP * P : (g + 1) * GROUP * P]
+            in_table_order = flipped[:].rearrange("d (k p) -> d p k", k=RUN)
+            columns = window[:, g * P * RUN : (g + 1) * P * RUN].rearrange("d (p k) -> d p k", k=RUN)
             if g % 2 == 0:
-                nc.vector.tensor_copy(columns, flipped[:])
+                nc.vector.tensor_copy(columns, in_table_order)
             else:
-                nc.scalar.copy(columns, flipped[:])
+                nc.scalar.copy(columns, in_table_order)
 
         for piece in range(N // PIECE):
             piece_offsets = offsets[:, piece * (PIECE // 16) : (piece + 1) * (PIECE // 16)]

@@ -7,6 +7,8 @@ PIECE = 512
 RUN = 4
 GROUPS = V // (P * RUN)
 
+WARM_UPS = 6
+
 BF16, F32, U16 = mybir.dt.bfloat16, mybir.dt.float32, mybir.dt.uint16
 
 FLOPS = 2 * D * (2 * D) * N
@@ -16,10 +18,17 @@ def tile_wsdmodel_kernel(tc, table, w_a, w_o, offs, out):
     nc = tc.nc
     with (
         tc.tile_pool(name="held", bufs=1) as held,
-        tc.tile_pool(name="staging", bufs=4) as staging,
+        tc.tile_pool(name="staging", bufs=2 * N // PIECE) as staging,
+        tc.psum_pool(name="warm_bank", bufs=1) as warm_bank,
         tc.psum_pool(name="flip_banks", bufs=4) as flip_banks,
-        tc.psum_pool(name="product_banks", bufs=2) as product_banks,
+        tc.psum_pool(name="product_banks", bufs=3) as product_banks,
     ):
+        zeros = held.tile([P, PIECE], BF16, name="zeros")
+        nc.vector.memset(zeros[:], 0.0)
+        unused = warm_bank.tile([P, PIECE], F32, name="unused")
+        for i in range(WARM_UPS):
+            nc.tensor.matmul(unused[:], zeros[:, 0:P], zeros[:], start=True, stop=True)
+
         offsets = held.tile([P, N // 16], U16, name="offsets")
         nc.sync.dma_start(offsets[:], offs)
 
@@ -29,13 +38,13 @@ def tile_wsdmodel_kernel(tc, table, w_a, w_o, offs, out):
             queue = nc.sync if g % 2 == 0 else nc.scalar
             queue.dma_start(words[:, g, :], table_runs[:, g, :])
 
+        weights_a = held.tile([D, D], BF16, name="weights_a")
+        nc.sync.dma_start(weights_a[:], w_a)
+        weights_o = held.tile([D, D], BF16, name="weights_o")
+        nc.scalar.dma_start(weights_o[:], w_o)
+
         identity = held.tile([P, P], BF16, name="identity")
         make_identity(nc, identity[:])
-
-        weights_a = held.tile([D, D], BF16, name="weights_a")
-        nc.gpsimd.dma_start(weights_a[:], w_a)
-        weights_o = held.tile([D, D], BF16, name="weights_o")
-        nc.gpsimd.dma_start(weights_o[:], w_o)
 
         window = held.tile([D, V], BF16, name="window")
         for g in range(GROUPS):
@@ -53,20 +62,16 @@ def tile_wsdmodel_kernel(tc, table, w_a, w_o, offs, out):
 
         for piece in range(N // PIECE):
             piece_offsets = offsets[:, piece * (PIECE // 16) : (piece + 1) * (PIECE // 16)]
-            piece_columns = slice(piece * PIECE, (piece + 1) * PIECE)
-
-            product_a = product_banks.tile([D, PIECE], F32, name="product_a")
-            nc.tensor.matmul(
-                product_a[:], weights_a[:], window[:].indirect(piece_offsets), start=True, stop=True
-            )
-            staged_a = staging.tile([D, PIECE], F32, name="staged_a")
-            nc.vector.tensor_copy(staged_a[:], product_a[:])
-            nc.sync.dma_start(out[0:D, piece_columns], staged_a[:])
-
-            product_o = product_banks.tile([D, PIECE], F32, name="product_o")
-            nc.tensor.matmul(
-                product_o[:], weights_o[:], window[:].indirect(piece_offsets), start=True, stop=True
-            )
-            staged_o = staging.tile([D, PIECE], F32, name="staged_o")
-            nc.scalar.copy(staged_o[:], product_o[:])
-            nc.scalar.dma_start(out[D : 2 * D, piece_columns], staged_o[:])
+            for half, weights in enumerate((weights_a, weights_o)):
+                product = product_banks.tile([D, PIECE], F32, name="product")
+                nc.tensor.matmul(
+                    product[:], weights[:], window[:].indirect(piece_offsets), start=True, stop=True
+                )
+                staged = staging.tile([D, PIECE], F32, name="staged")
+                out_block = out[half * D : (half + 1) * D, piece * PIECE : (piece + 1) * PIECE]
+                if half == 0:
+                    nc.vector.tensor_copy(staged[:], product[:])
+                    nc.sync.dma_start(out_block, staged[:])
+                else:
+                    nc.scalar.copy(staged[:], product[:])
+                    nc.scalar.dma_start(out_block, staged[:])

@@ -4,6 +4,8 @@ from concourse.masks import make_identity
 V, D, N = 4096, 128, 2048
 P = 128
 PIECE = 512
+PIECES = (512, 512, 512, 256, 128, 128)
+assert sum(PIECES) == N and max(PIECES) == PIECE
 RUN = 4
 GROUPS = V // (P * RUN)
 
@@ -18,7 +20,7 @@ def tile_wsdmodel_kernel(tc, table, w_a, w_o, offs, out):
     nc = tc.nc
     with (
         tc.tile_pool(name="held", bufs=1) as held,
-        tc.tile_pool(name="staging", bufs=2 * N // PIECE) as staging,
+        tc.tile_pool(name="staging", bufs=2 * len(PIECES)) as staging,
         tc.psum_pool(name="warm_bank", bufs=1) as warm_bank,
         tc.psum_pool(name="flip_banks", bufs=4) as flip_banks,
         tc.psum_pool(name="product_banks", bufs=3) as product_banks,
@@ -60,18 +62,24 @@ def tile_wsdmodel_kernel(tc, table, w_a, w_o, offs, out):
             else:
                 nc.scalar.copy(columns, in_table_order)
 
-        for piece in range(N // PIECE):
-            piece_offsets = offsets[:, piece * (PIECE // 16) : (piece + 1) * (PIECE // 16)]
+        first = 0
+        for size in PIECES:
+            piece_offsets = offsets[:, first // 16 : (first + size) // 16]
             for half, weights in enumerate((weights_a, weights_o)):
                 product = product_banks.tile([D, PIECE], F32, name="product")
                 nc.tensor.matmul(
-                    product[:], weights[:], window[:].indirect(piece_offsets), start=True, stop=True
+                    product[:, 0:size],
+                    weights[:],
+                    window[:].indirect(piece_offsets),
+                    start=True,
+                    stop=True,
                 )
                 staged = staging.tile([D, PIECE], F32, name="staged")
-                out_block = out[half * D : (half + 1) * D, piece * PIECE : (piece + 1) * PIECE]
+                out_block = out[half * D : (half + 1) * D, first : first + size]
                 if half == 0:
-                    nc.vector.tensor_copy(staged[:], product[:])
-                    nc.sync.dma_start(out_block, staged[:])
+                    nc.vector.tensor_copy(staged[:, 0:size], product[:, 0:size])
+                    nc.sync.dma_start(out_block, staged[:, 0:size])
                 else:
-                    nc.scalar.copy(staged[:], product[:])
-                    nc.scalar.dma_start(out_block, staged[:])
+                    nc.scalar.copy(staged[:, 0:size], product[:, 0:size])
+                    nc.scalar.dma_start(out_block, staged[:, 0:size])
+            first += size

@@ -4,8 +4,6 @@ from concourse.masks import make_identity
 V, D, N = 4096, 128, 2048
 P = 128
 PIECE = 512
-PIECES = (512, 512, 512, 256, 128, 128)
-assert sum(PIECES) == N and max(PIECES) == PIECE
 RUN = 4
 GROUPS = V // (P * RUN)
 
@@ -20,14 +18,12 @@ def tile_wsdmodel_kernel(tc, table, w_a, w_o, offs, out):
     nc = tc.nc
     with (
         tc.tile_pool(name="held", bufs=1) as held,
-        tc.tile_pool(name="staging", bufs=2 * len(PIECES)) as staging,
-        tc.psum_pool(name="warm_bank", bufs=1) as warm_bank,
-        tc.psum_pool(name="flip_banks", bufs=4) as flip_banks,
-        tc.psum_pool(name="product_banks", bufs=3) as product_banks,
+        tc.tile_pool(name="staging", bufs=2 * N // PIECE) as staging,
+        tc.psum_pool(name="banks", bufs=8) as banks,
     ):
         zeros = held.tile([P, PIECE], BF16, name="zeros")
         nc.vector.memset(zeros[:], 0.0)
-        unused = warm_bank.tile([P, PIECE], F32, name="unused")
+        unused = banks.tile([P, PIECE], F32, name="unused", tag="bank")
         for i in range(WARM_UPS):
             nc.tensor.matmul(unused[:], zeros[:, 0:P], zeros[:], start=True, stop=True)
 
@@ -50,7 +46,7 @@ def tile_wsdmodel_kernel(tc, table, w_a, w_o, offs, out):
 
         window = held.tile([D, V], BF16, name="window")
         for g in range(GROUPS):
-            flipped = flip_banks.tile([D, RUN * P], BF16, name="flipped")
+            flipped = banks.tile([D, RUN * P], BF16, name="flipped", tag="bank")
             for k in range(RUN):
                 nc.tensor.transpose(
                     flipped[:, k * P : (k + 1) * P], words[:, g, k * D : (k + 1) * D], identity[:]
@@ -62,24 +58,18 @@ def tile_wsdmodel_kernel(tc, table, w_a, w_o, offs, out):
             else:
                 nc.scalar.copy(columns, in_table_order)
 
-        first = 0
-        for size in PIECES:
-            piece_offsets = offsets[:, first // 16 : (first + size) // 16]
+        for piece in range(N // PIECE):
+            piece_offsets = offsets[:, piece * (PIECE // 16) : (piece + 1) * (PIECE // 16)]
             for half, weights in enumerate((weights_a, weights_o)):
-                product = product_banks.tile([D, PIECE], F32, name="product")
+                product = banks.tile([D, PIECE], F32, name="product", tag="bank")
                 nc.tensor.matmul(
-                    product[:, 0:size],
-                    weights[:],
-                    window[:].indirect(piece_offsets),
-                    start=True,
-                    stop=True,
+                    product[:], weights[:], window[:].indirect(piece_offsets), start=True, stop=True
                 )
                 staged = staging.tile([D, PIECE], F32, name="staged")
-                out_block = out[half * D : (half + 1) * D, first : first + size]
+                out_block = out[half * D : (half + 1) * D, piece * PIECE : (piece + 1) * PIECE]
                 if half == 0:
-                    nc.vector.tensor_copy(staged[:, 0:size], product[:, 0:size])
-                    nc.sync.dma_start(out_block, staged[:, 0:size])
+                    nc.vector.tensor_copy(staged[:], product[:])
+                    nc.sync.dma_start(out_block, staged[:])
                 else:
-                    nc.scalar.copy(staged[:, 0:size], product[:, 0:size])
-                    nc.scalar.dma_start(out_block, staged[:, 0:size])
-            first += size
+                    nc.scalar.copy(staged[:], product[:])
+                    nc.scalar.dma_start(out_block, staged[:])

@@ -7,7 +7,7 @@ PIECE = 512
 RUN = 4
 GROUPS = V // (P * RUN)
 
-WARM_UPS = 6
+WARM_UPS = 4
 
 BF16, F32, U16 = mybir.dt.bfloat16, mybir.dt.float32, mybir.dt.uint16
 

@@ -33,11 +33,10 @@ def tile_wsdmodel_kernel(tc, table, w_a, w_o, offs, out):
         words = held.tile([P, GROUPS, RUN * D], BF16, name="words")
         table_runs = table.rearrange("(g p k) d -> p g (k d)", p=P, k=RUN)
         for g in range(GROUPS):
-            queue = nc.sync if g % 2 == 0 else nc.scalar
-            queue.dma_start(words[:, g, :], table_runs[:, g, :])
+            nc.sync.dma_start(words[:, g, :], table_runs[:, g, :])
 
         weights_a = held.tile([D, D], BF16, name="weights_a")
-        nc.sync.dma_start(weights_a[:], w_a)
+        nc.scalar.dma_start(weights_a[:], w_a)
         weights_o = held.tile([D, D], BF16, name="weights_o")
         nc.scalar.dma_start(weights_o[:], w_o)
 

import concourse.mybir as mybir
from concourse.masks import make_identity

V, D, N = 4096, 128, 2048
P = 128
PIECE = 512
RUN = 4
GROUPS = V // (P * RUN)

WARM_UPS = 4

BF16, F32, U16 = mybir.dt.bfloat16, mybir.dt.float32, mybir.dt.uint16

FLOPS = 2 * D * (2 * D) * N


def tile_wsdmodel_kernel(tc, table, w_a, w_o, offs, out):
    nc = tc.nc
    with (
        tc.tile_pool(name="held", bufs=1) as held,
        tc.tile_pool(name="staging", bufs=2 * N // PIECE) as staging,
        tc.psum_pool(name="banks", bufs=8) as banks,
    ):
        zeros = held.tile([P, PIECE], BF16, name="zeros")
        nc.vector.memset(zeros[:], 0.0)
        unused = banks.tile([P, PIECE], F32, name="unused", tag="bank")
        for i in range(WARM_UPS):
            nc.tensor.matmul(unused[:], zeros[:, 0:P], zeros[:], start=True, stop=True)

        offsets = held.tile([P, N // 16], U16, name="offsets")
        nc.sync.dma_start(offsets[:], offs)

        words = held.tile([P, GROUPS, RUN * D], BF16, name="words")
        table_runs = table.rearrange("(g p k) d -> p g (k d)", p=P, k=RUN)
        for g in range(GROUPS):
            nc.sync.dma_start(words[:, g, :], table_runs[:, g, :])

        weights_a = held.tile([D, D], BF16, name="weights_a")
        nc.scalar.dma_start(weights_a[:], w_a)
        weights_o = held.tile([D, D], BF16, name="weights_o")
        nc.scalar.dma_start(weights_o[:], w_o)

        identity = held.tile([P, P], BF16, name="identity")
        make_identity(nc, identity[:])

        window = held.tile([D, V], BF16, name="window")
        for g in range(GROUPS):
            flipped = banks.tile([D, RUN * P], BF16, name="flipped", tag="bank")
            for k in range(RUN):
                nc.tensor.transpose(
                    flipped[:, k * P : (k + 1) * P], words[:, g, k * D : (k + 1) * D], identity[:]
                )
            in_table_order = flipped[:].rearrange("d (k p) -> d p k", k=RUN)
            columns = window[:, g * P * RUN : (g + 1) * P * RUN].rearrange("d (p k) -> d p k", k=RUN)
            if g % 2 == 0:
                nc.vector.tensor_copy(columns, in_table_order)
            else:
                nc.scalar.copy(columns, in_table_order)

        for piece in range(N // PIECE):
            piece_offsets = offsets[:, piece * (PIECE // 16) : (piece + 1) * (PIECE // 16)]
            for half, weights in enumerate((weights_a, weights_o)):
                product = banks.tile([D, PIECE], F32, name="product", tag="bank")
                nc.tensor.matmul(
                    product[:], weights[:], window[:].indirect(piece_offsets), start=True, stop=True
                )
                staged = staging.tile([D, PIECE], F32, name="staged")
                out_block = out[half * D : (half + 1) * D, piece * PIECE : (piece + 1) * PIECE]
                if half == 0:
                    nc.vector.tensor_copy(staged[:], product[:])
                    nc.sync.dma_start(out_block, staged[:])
                else:
                    nc.scalar.copy(staged[:], product[:])
                    nc.scalar.dma_start(out_block, staged[:])
